import numpy as np
import ml_dtypes


def mxq(x, axis, fmt="e4m3"):
    dtype, down = {"e4m3": (ml_dtypes.float8_e4m3fn, 7), "e5m2": (ml_dtypes.float8_e5m2, 14)}[fmt]
    v = np.moveaxis(np.asarray(x, np.float32).astype(ml_dtypes.bfloat16).astype(np.float64), axis, -1)
    blocks = v.reshape(v.shape[:-1] + (-1, 32))
    amax = np.abs(blocks).max(-1, keepdims=True)
    byte = np.maximum(np.where(amax > 0, np.frexp(amax)[1] - 1 + 127, 0) - down, 1)
    scale = np.exp2(byte - 127.0)
    codes = (blocks / scale).astype(np.float32).astype(dtype).astype(np.float64)
    return np.moveaxis((codes * scale).reshape(v.shape), -1, axis)


WIDE = False


def mx_kscale(k):
    if not WIDE:
        return np.ones(k)
    levels = np.array([10, -10, 5, -5, 0])
    if k % 512:
        return np.exp2(np.random.permutation(np.resize(levels, k // 32))).repeat(32)
    a = np.empty((k // 512, 16))
    for p in range(k // 512):
        a[p, :8] = np.random.permutation(np.resize(levels, 8))
        for g in range(8):
            far = levels[np.abs(levels - a[p, g]) >= 10]
            a[p, g + 8] = far[np.random.randint(len(far))]
    return np.exp2(a.ravel()).repeat(32)


BF16 = ml_dtypes.bfloat16


def bf(x):
    return np.asarray(x, np.float32).astype(BF16)


def f64(x):
    return np.asarray(x).astype(np.float64)


N, T, H, P0, P1, C0, NC, V0, V1 = 4, 1024, 1024, 512, 128, 20000, 2, 1024, 12288


def setup_inputs():
    s, t = mx_kscale(H), mx_kscale(P0)
    return {"x": bf(np.random.standard_normal((N, T, H)) * s),
            "tail_proj_0": bf(np.random.standard_normal((H, P0)) / np.sqrt(H) / s[:, None] * t),
            "tail_w_0": bf(np.random.standard_normal((P0, V0)) * 2.0 / np.sqrt(P0) / t[:, None]),
            "cluster_prob": bf(0.05 + 0.55 * np.random.random((N, T))[..., None])}


def reference(x, tail_proj_0, tail_w_0, cluster_prob):
    h = mxq(f64(x), 2, "e4m3") @ mxq(f64(tail_proj_0), 0, "e4m3")
    logits = mxq(h, 2, "e4m3") @ mxq(f64(tail_w_0), 0, "e4m3")
    e = np.exp(logits - logits.max(-1, keepdims=True))
    return e / e.sum(-1, keepdims=True) * f64(cluster_prob)

@@ -1,0 +1,293 @@
+from contextlib import ExitStack
+
+import concourse.mybir as mybir
+from concourse.masks import make_identity
+
+F32 = mybir.dt.float32
+BF16 = mybir.dt.bfloat16
+U32 = mybir.dt.uint32
+U8 = mybir.dt.uint8
+FP8X4 = mybir.dt.float8_e4m3fn_x4
+ALU = mybir.AluOpType
+ACT = mybir.ActivationFunctionType
+AX = mybir.AxisListType
+
+P = 128
+TOKENS = 4096
+H = 1024
+P0 = 512
+V0 = 1024
+TILES = TOKENS // P
+PAIRS = TILES // 2
+
+FLOPS = 2 * TOKENS * H * P0 + 2 * TOKENS * P0 * V0
+
+MANUAL = False
+QUADS = 8
+S_XC = 3
+S_HC = 3
+DELAY = 2
+TAIL = 6
+EARLY = 2
+GTAIL = 0
+
+
+def tile_adaptiveinputsoftmax_pa_t_kernel(tc, x, tail_proj_0, tail_w_0, cluster_prob, out):
+    nc = tc.nc
+    with ExitStack() as ctx:
+        const = ctx.enter_context(tc.tile_pool(name="const", bufs=1))
+        xg_pool = ctx.enter_context(tc.tile_pool(name="xg_pool", bufs=2))
+        xc_pool = ctx.enter_context(tc.tile_pool(name="xc_pool", bufs=2))
+        hg_pool = ctx.enter_context(tc.tile_pool(name="hg_pool", bufs=2))
+        e_pool = ctx.enter_context(tc.tile_pool(name="e_pool", bufs=5))
+        st_pool = ctx.enter_context(tc.tile_pool(name="st_pool", bufs=8))
+        ps_pool = ctx.enter_context(tc.psum_pool(name="ps_pool", bufs=8))
+        if MANUAL:
+            ctx.enter_context(tc.manual_schedule())
+
+        x_rows = x.flatten_outer_dims().rearrange("(p i) k -> p (i k)", i=TILES)
+        out_rows = out.flatten_outer_dims().rearrange("(p i) v -> p (i v)", i=TILES)
+        prob_rows = cluster_prob.rearrange("n t o -> (n t o)").rearrange("(p i) -> p i", i=TILES)
+
+        ident = const.tile([P, P], F32, name="ident")
+        make_identity(nc, ident[:])
+        warm_in = const.tile([P, 1], F32, name="warm_in")
+        warm_out = const.tile([P, 1], F32, name="warm_out")
+        nc.vector.memset(warm_in[:], 0.0)
+        nc.scalar.activation(out=warm_out[:], in_=warm_in[:], func=ACT.Exp)
+
+        p_raw = const.tile([P, 4096], BF16, name="p_raw")
+        p_grp = const.tile([P, 4096], BF16, name="p_grp", align_bytes=64)
+        p_cod = const.tile([P, 1024], U32, name="p_cod", align_bytes=64)
+        p_scl = const.tile([P, 1024], U8, name="p_scl", align_bytes=64)
+        w_raw = const.tile([P, 4096], BF16, name="w_raw")
+        w_grp = const.tile([P, 4096], BF16, name="w_grp", align_bytes=64)
+        w_cod = const.tile([P, 1024], U32, name="w_cod", align_bytes=64)
+        w_scl = const.tile([P, 1024], U8, name="w_scl", align_bytes=64)
+        prob_bf = const.tile([P, TILES], BF16, name="prob_bf")
+        prob = const.tile([P, TILES], F32, name="prob")
+        h_cod = const.tile([P, TOKENS], U32, name="h_cod", align_bytes=64)
+        h_scl = const.tile([P, TOKENS], U8, name="h_scl", align_bytes=64)
+        x_sb = [const.tile([P, 4096], BF16, name="x_sb%d" % g) for g in range(8)]
+
+        for c in range(2):
+            nc.sync.dma_start(
+                out=p_raw[:, 2048 * c : 2048 * (c + 1)],
+                in_=tail_proj_0[512 * c : 512 * (c + 1), :].rearrange("(p j) n -> p (j n)", j=4),
+            )
+        for a in range(2):
+            nc.sync.dma_start(out=x_sb[0][:, 2048 * a : 2048 * (a + 1)], in_=x_rows[:, 2048 * a : 2048 * (a + 1)])
+        for g in range(1, 8):
+            nc.sync.dma_start(out=x_sb[g][:], in_=x_rows[:, 4096 * g : 4096 * (g + 1)])
+            if g == 1:
+                nc.sync.dma_start(
+                    out=w_raw[:].rearrange("p (t n) -> p t n", t=4),
+                    in_=tail_w_0.rearrange("(p t) n -> p t n", t=4),
+                )
+                nc.sync.dma_start(out=prob_bf[:], in_=prob_rows)
+
+        def prepare_proj():
+            for c in range(2):
+                cols = slice(2048 * c, 2048 * (c + 1))
+                nc.vector.tensor_copy(
+                    out=p_grp[:, cols].rearrange("p (t m j) -> p t m j", t=4, j=4),
+                    in_=p_raw[:, cols].rearrange("p (j m t) -> p t m j", j=4, t=4),
+                )
+            for c in range(2):
+                nc.vector.quantize_mx(
+                    out=p_cod[:, 512 * c : 512 * (c + 1)].bitcast(FP8X4),
+                    scales=p_scl[:, 512 * c : 512 * (c + 1)],
+                    in_=p_grp[:, 2048 * c : 2048 * (c + 1)],
+                )
+
+        def prepare_w():
+            planes = w_raw[:].rearrange("p (t n) -> p t n", t=4)
+            for v in range(2):
+                nc.vector.tensor_copy(
+                    out=w_grp[:, 2048 * v : 2048 * (v + 1)].rearrange("p (a i t) -> p a t i", i=4, t=4),
+                    in_=planes[:, :, 512 * v : 512 * (v + 1)].rearrange("p t (a i) -> p a t i", i=4),
+                )
+            for v in range(2):
+                nc.vector.quantize_mx(
+                    out=w_cod[:, 512 * v : 512 * (v + 1)].bitcast(FP8X4),
+                    scales=w_scl[:, 512 * v : 512 * (v + 1)],
+                    in_=w_grp[:, 2048 * v : 2048 * (v + 1)],
+                )
+            nc.vector.tensor_copy(out=prob[:], in_=prob_bf[:])
+
+        xt_of = {}
+        xg_of = {}
+        xc_of = {}
+        ht_of = {}
+        hg_of = {}
+        lg_of = {}
+        mx_of = {}
+        e_of = {}
+        sm_of = {}
+        rc_of = {}
+
+        def transposes(g):
+            words = x_sb[g][:].bitcast(F32)
+            for j in range(4):
+                xt = ps_pool.tile([P, 512], F32, name="bank")
+                for s in range(4):
+                    first = 512 * j + 256 * (s // 2) + s % 2
+                    nc.tensor.transpose(xt[:, P * s : P * (s + 1)], words[:, first : first + 255 : 2], ident[:])
+                xt_of[4 * g + j] = xt
+
+        def copy_x(g):
+            xg = xg_pool.tile([P, 4096], BF16, name="xg", align_bytes=64)
+            xg_of[g] = xg
+            for j in range(4):
+                copy = nc.scalar.copy if j < S_XC else nc.vector.tensor_copy
+                copy(
+                    out=xg[:, 1024 * j : 1024 * (j + 1)].bitcast(F32).rearrange("p (c r u) -> p c r u", c=2, u=2),
+                    in_=xt_of[4 * g + j][:].rearrange("p (c u r) -> p c r u", c=2, u=2),
+                )
+
+        def quantise_x(g):
+            cod = xc_pool.tile([P, 1024], U32, name="x_cod", align_bytes=64)
+            scl = xc_pool.tile([P, 1024], U8, name="x_scl", align_bytes=64)
+            for a in range(2):
+                nc.vector.quantize_mx(
+                    out=cod[:, 512 * a : 512 * (a + 1)].bitcast(FP8X4),
+                    scales=scl[:, 512 * a : 512 * (a + 1)],
+                    in_=xg_of[g][:, 2048 * a : 2048 * (a + 1)],
+                )
+            xc_of[g] = (cod, scl)
+
+        def stage1(g):
+            cod, scl = xc_of[g]
+            for j in range(4):
+                ht = ps_pool.tile([P, 512], F32, name="bank")
+                ht_of[4 * g + j] = ht
+                for t in range(4):
+                    for c in range(2):
+                        wcols = slice(512 * c + P * t, 512 * c + P * (t + 1))
+                        xcols = slice(256 * j + P * c, 256 * j + P * (c + 1))
+                        nc.tensor.matmul_mx(
+                            out=ht[:, P * t : P * (t + 1)],
+                            lhsT=p_cod[:, wcols].bitcast(FP8X4),
+                            lhsT_scale=p_scl[:, wcols],
+                            rhs=cod[:, xcols].bitcast(FP8X4),
+                            rhs_scale=scl[:, xcols],
+                            start=(c == 0),
+                            stop=(c == 1),
+                        )
+
+        def copy_h(g):
+            hg = hg_pool.tile([P, 2048], BF16, name="hg", align_bytes=64)
+            hg_of[g] = hg
+            for j in range(4):
+                copy = nc.scalar.copy if (j < S_HC or g == QUADS - 1) else nc.vector.tensor_copy
+                copy(
+                    out=hg[:, 512 * j : 512 * (j + 1)].rearrange("p (r t) -> p r t", t=4),
+                    in_=ht_of[4 * g + j][:].rearrange("p (t r) -> p r t", t=4),
+                )
+
+        def quantise_h(g):
+            cols = slice(512 * g, 512 * (g + 1))
+            nc.vector.quantize_mx(out=h_cod[:, cols].bitcast(FP8X4), scales=h_scl[:, cols], in_=hg_of[g][:])
+
+        def stage2(i):
+            for v in range(2):
+                lg = ps_pool.tile([P, 512], F32, name="bank")
+                nc.tensor.matmul_mx(
+                    out=lg[:],
+                    lhsT=h_cod[:, P * i : P * (i + 1)].bitcast(FP8X4),
+                    lhsT_scale=h_scl[:, P * i : P * (i + 1)],
+                    rhs=w_cod[:, 512 * v : 512 * (v + 1)].bitcast(FP8X4),
+                    rhs_scale=w_scl[:, 512 * v : 512 * (v + 1)],
+                    start=True,
+                    stop=True,
+                )
+                lg_of[(i, v)] = lg
+
+        def row_max(i):
+            mx = st_pool.tile([P, 4], F32, name="mx")
+            mx_of[i] = mx
+            for v in range(2):
+                nc.vector.tensor_reduce(out=mx[:, v : v + 1], in_=lg_of[(i, v)][:], axis=AX.X, op=ALU.max)
+            nc.vector.tensor_reduce(out=mx[:, 2:3], in_=mx[:, 0:2], axis=AX.X, op=ALU.max, negate=True)
+
+        def exponent(i):
+            q, a = divmod(i, 2)
+            if a == 0:
+                e = e_pool.tile([P, 2048], F32, name="e")
+                sm = st_pool.tile([P, 4], F32, name="sm")
+                rc = st_pool.tile([P, 4], F32, name="rc")
+                e_of[q] = e
+                sm_of[q] = sm
+                rc_of[q] = rc
+            for v in range(2):
+                first = 1024 * a + 512 * v
+                nc.scalar.activation(
+                    out=e_of[q][:, first : first + 512],
+                    in_=lg_of[(i, v)][:],
+                    func=ACT.Exp,
+                    bias=mx_of[i][:, 2:3],
+                    scale=1.0,
+                    accum_out=sm_of[q][:, 2 * a + v : 2 * a + v + 1],
+                )
+
+        def finish(q, halves, engine):
+            lo, n = halves[0], len(halves)
+            sm = sm_of[q]
+            rc = rc_of[q]
+            nc.vector.tensor_reduce(
+                out=rc[:, lo : lo + n],
+                in_=sm[:, 2 * lo : 2 * (lo + n)].rearrange("p (a v) -> p a v", v=2),
+                axis=AX.X,
+                op=ALU.add,
+            )
+            nc.vector.reciprocal(out=rc[:, 2 + lo : 2 + lo + n], in_=rc[:, lo : lo + n])
+            for a in halves:
+                i = 2 * q + a
+                part = e_of[q][:, 1024 * a : 1024 * (a + 1)]
+                engine.tensor_scalar(
+                    out=part,
+                    in0=part,
+                    scalar1=rc[:, 2 + a : 3 + a],
+                    scalar2=prob[:, i : i + 1],
+                    op0=ALU.mult,
+                    op1=ALU.mult,
+                )
+                nc.sync.dma_start(out=out_rows[:, 1024 * i : 1024 * (i + 1)], in_=part)
+
+        def back_end(i):
+            if i < TILES:
+                stage2(i)
+                row_max(i)
+                exponent(i)
+            if i == EARLY + 1:
+                quantise_h(QUADS - 1)
+            d = i - DELAY
+            if d >= 0 and d % 2 == 1 and d < TILES - TAIL:
+                finish(d // 2, [0, 1], nc.gpsimd)
+            if d == TILES - TAIL and d % 2 == 0 and GTAIL:
+                finish(d // 2, [0], nc.gpsimd)
+
+        prepare_proj()
+        transposes(0)
+        copy_x(0)
+        quantise_x(0)
+        for g in range(QUADS):
+            if g + 1 < QUADS:
+                transposes(g + 1)
+            else:
+                for i in range(EARLY):
+                    back_end(i)
+            stage1(g)
+            if g + 1 < QUADS:
+                copy_x(g + 1)
+                quantise_x(g + 1)
+            if g == 1:
+                prepare_w()
+            copy_h(g)
+            if g + 1 < QUADS:
+                quantise_h(g)
+        for i in range(EARLY, TILES + DELAY):
+            back_end(i)
+            if i == TILES - 1:
+                for d in range(TILES - TAIL + GTAIL, TILES):
+                    finish(d // 2, [d % 2], nc.vector)

@@ -22,39 +22,24 @@ PAIRS = TILES // 2
 
 FLOPS = 2 * TOKENS * H * P0 + 2 * TOKENS * P0 * V0
 
-MANUAL = False
-QUADS = 8
-S_XC = 3
-S_HC = 3
-DELAY = 2
-TAIL = 6
-EARLY = 2
-GTAIL = 0
-
 
 def tile_adaptiveinputsoftmax_pa_t_kernel(tc, x, tail_proj_0, tail_w_0, cluster_prob, out):
     nc = tc.nc
     with ExitStack() as ctx:
         const = ctx.enter_context(tc.tile_pool(name="const", bufs=1))
-        xg_pool = ctx.enter_context(tc.tile_pool(name="xg_pool", bufs=2))
-        xc_pool = ctx.enter_context(tc.tile_pool(name="xc_pool", bufs=2))
-        hg_pool = ctx.enter_context(tc.tile_pool(name="hg_pool", bufs=2))
+        xg_pool = ctx.enter_context(tc.tile_pool(name="xg_pool", bufs=3))
+        xc_pool = ctx.enter_context(tc.tile_pool(name="xc_pool", bufs=3))
+        hg_pool = ctx.enter_context(tc.tile_pool(name="hg_pool", bufs=3))
         e_pool = ctx.enter_context(tc.tile_pool(name="e_pool", bufs=5))
         st_pool = ctx.enter_context(tc.tile_pool(name="st_pool", bufs=8))
-        ps_pool = ctx.enter_context(tc.psum_pool(name="ps_pool", bufs=8))
-        if MANUAL:
-            ctx.enter_context(tc.manual_schedule())
+        xt_pool = ctx.enter_context(tc.psum_pool(name="xt_pool", bufs=2))
+        ht_pool = ctx.enter_context(tc.psum_pool(name="ht_pool", bufs=2))
+        lg_pool = ctx.enter_context(tc.psum_pool(name="lg_pool", bufs=4))
+        ctx.enter_context(tc.manual_schedule())
 
         x_rows = x.flatten_outer_dims().rearrange("(p i) k -> p (i k)", i=TILES)
         out_rows = out.flatten_outer_dims().rearrange("(p i) v -> p (i v)", i=TILES)
         prob_rows = cluster_prob.rearrange("n t o -> (n t o)").rearrange("(p i) -> p i", i=TILES)
-
-        ident = const.tile([P, P], F32, name="ident")
-        make_identity(nc, ident[:])
-        warm_in = const.tile([P, 1], F32, name="warm_in")
-        warm_out = const.tile([P, 1], F32, name="warm_out")
-        nc.vector.memset(warm_in[:], 0.0)
-        nc.scalar.activation(out=warm_out[:], in_=warm_in[:], func=ACT.Exp)
 
         p_raw = const.tile([P, 4096], BF16, name="p_raw")
         p_grp = const.tile([P, 4096], BF16, name="p_grp", align_bytes=64)
@@ -68,52 +53,54 @@ def tile_adaptiveinputsoftmax_pa_t_kernel(tc, x, tail_proj_0, tail_w_0, cluster_
         prob = const.tile([P, TILES], F32, name="prob")
         h_cod = const.tile([P, TOKENS], U32, name="h_cod", align_bytes=64)
         h_scl = const.tile([P, TOKENS], U8, name="h_scl", align_bytes=64)
-        x_sb = [const.tile([P, 4096], BF16, name="x_sb%d" % g) for g in range(8)]
+        x_sb = [const.tile([P, 2048], BF16, name="x_sb%d" % g) for g in range(PAIRS)]
 
         for c in range(2):
             nc.sync.dma_start(
                 out=p_raw[:, 2048 * c : 2048 * (c + 1)],
                 in_=tail_proj_0[512 * c : 512 * (c + 1), :].rearrange("(p j) n -> p (j n)", j=4),
             )
-        for a in range(2):
-            nc.sync.dma_start(out=x_sb[0][:, 2048 * a : 2048 * (a + 1)], in_=x_rows[:, 2048 * a : 2048 * (a + 1)])
-        for g in range(1, 8):
-            nc.sync.dma_start(out=x_sb[g][:], in_=x_rows[:, 4096 * g : 4096 * (g + 1)])
-            if g == 1:
-                nc.sync.dma_start(
-                    out=w_raw[:].rearrange("p (t n) -> p t n", t=4),
-                    in_=tail_w_0.rearrange("(p t) n -> p t n", t=4),
-                )
+        for g in range(PAIRS):
+            nc.sync.dma_start(out=x_sb[g][:], in_=x_rows[:, 2048 * g : 2048 * (g + 1)])
+            if g == 2:
+                nc.sync.dma_start(out=w_raw[:], in_=tail_w_0.rearrange("(p j) n -> p (j n)", j=4))
                 nc.sync.dma_start(out=prob_bf[:], in_=prob_rows)
 
-        def prepare_proj():
-            for c in range(2):
-                cols = slice(2048 * c, 2048 * (c + 1))
-                nc.vector.tensor_copy(
-                    out=p_grp[:, cols].rearrange("p (t m j) -> p t m j", t=4, j=4),
-                    in_=p_raw[:, cols].rearrange("p (j m t) -> p t m j", j=4, t=4),
-                )
-            for c in range(2):
-                nc.vector.quantize_mx(
-                    out=p_cod[:, 512 * c : 512 * (c + 1)].bitcast(FP8X4),
-                    scales=p_scl[:, 512 * c : 512 * (c + 1)],
-                    in_=p_grp[:, 2048 * c : 2048 * (c + 1)],
-                )
+        ident = const.tile([P, P], F32, name="ident")
+        make_identity(nc, ident[:])
+        warm_in = const.tile([P, 1], F32, name="warm_in")
+        warm_out = const.tile([P, 1], F32, name="warm_out")
+        nc.vector.memset(warm_in[:], 0.0)
+        nc.scalar.activation(out=warm_out[:], in_=warm_in[:], func=ACT.Exp)
 
-        def prepare_w():
-            planes = w_raw[:].rearrange("p (t n) -> p t n", t=4)
-            for v in range(2):
-                nc.vector.tensor_copy(
-                    out=w_grp[:, 2048 * v : 2048 * (v + 1)].rearrange("p (a i t) -> p a t i", i=4, t=4),
-                    in_=planes[:, :, 512 * v : 512 * (v + 1)].rearrange("p t (a i) -> p a t i", i=4),
-                )
-            for v in range(2):
-                nc.vector.quantize_mx(
-                    out=w_cod[:, 512 * v : 512 * (v + 1)].bitcast(FP8X4),
-                    scales=w_scl[:, 512 * v : 512 * (v + 1)],
-                    in_=w_grp[:, 2048 * v : 2048 * (v + 1)],
-                )
-            nc.vector.tensor_copy(out=prob[:], in_=prob_bf[:])
+        def group_proj(c, copy, slots):
+            cols = slice(2048 * c, 2048 * (c + 1))
+            lo, hi = slots
+            copy(
+                out=p_grp[:, cols].rearrange("p (t m j) -> p t m j", t=4, j=4)[:, lo:hi],
+                in_=p_raw[:, cols].rearrange("p (j m t) -> p t m j", j=4, t=4)[:, lo:hi],
+            )
+
+        def quantise_proj(c):
+            nc.vector.quantize_mx(
+                out=p_cod[:, 512 * c : 512 * (c + 1)].bitcast(FP8X4),
+                scales=p_scl[:, 512 * c : 512 * (c + 1)],
+                in_=p_grp[:, 2048 * c : 2048 * (c + 1)],
+            )
+
+        def group_w(v, copy):
+            rows = w_raw[:].rearrange("p (j n) -> p j n", j=4)
+            copy(
+                out=w_grp[:, 2048 * v : 2048 * (v + 1)].rearrange("p (a i j) -> p a j i", i=4, j=4),
+                in_=rows[:, :, 512 * v : 512 * (v + 1)].rearrange("p j (a i) -> p a j i", i=4),
+            )
+
+        def quantise_w(v):
+            nc.vector.quantize_mx(
+                out=w_cod[:, 512 * v : 512 * (v + 1)].bitcast(FP8X4),
+                scales=w_scl[:, 512 * v : 512 * (v + 1)],
+                in_=w_grp[:, 2048 * v : 2048 * (v + 1)],
+            )
 
         xt_of = {}
         xg_of = {}
@@ -124,47 +111,39 @@ def tile_adaptiveinputsoftmax_pa_t_kernel(tc, x, tail_proj_0, tail_w_0, cluster_
         mx_of = {}
         e_of = {}
         sm_of = {}
-        rc_of = {}
 
-        def transposes(g):
-            words = x_sb[g][:].bitcast(F32)
-            for j in range(4):
-                xt = ps_pool.tile([P, 512], F32, name="bank")
-                for s in range(4):
-                    first = 512 * j + 256 * (s // 2) + s % 2
-                    nc.tensor.transpose(xt[:, P * s : P * (s + 1)], words[:, first : first + 255 : 2], ident[:])
-                xt_of[4 * g + j] = xt
-
-        def copy_x(g):
-            xg = xg_pool.tile([P, 4096], BF16, name="xg", align_bytes=64)
-            xg_of[g] = xg
-            for j in range(4):
-                copy = nc.scalar.copy if j < S_XC else nc.vector.tensor_copy
-                copy(
-                    out=xg[:, 1024 * j : 1024 * (j + 1)].bitcast(F32).rearrange("p (c r u) -> p c r u", c=2, u=2),
-                    in_=xt_of[4 * g + j][:].rearrange("p (c u r) -> p c r u", c=2, u=2),
-                )
-
-        def quantise_x(g):
-            cod = xc_pool.tile([P, 1024], U32, name="x_cod", align_bytes=64)
-            scl = xc_pool.tile([P, 1024], U8, name="x_scl", align_bytes=64)
+        def transposes(q):
+            words = x_sb[q][:].bitcast(F32)
             for a in range(2):
-                nc.vector.quantize_mx(
-                    out=cod[:, 512 * a : 512 * (a + 1)].bitcast(FP8X4),
-                    scales=scl[:, 512 * a : 512 * (a + 1)],
-                    in_=xg_of[g][:, 2048 * a : 2048 * (a + 1)],
-                )
-            xc_of[g] = (cod, scl)
+                xt = xt_pool.tile([P, 512], F32, name="xt")
+                for s in range(4):
+                    first = 512 * a + 256 * (s // 2) + s % 2
+                    nc.tensor.transpose(xt[:, P * s : P * (s + 1)], words[:, first : first + 255 : 2], ident[:])
+                xt_of[(q, a)] = xt
 
-        def stage1(g):
-            cod, scl = xc_of[g]
-            for j in range(4):
-                ht = ps_pool.tile([P, 512], F32, name="bank")
-                ht_of[4 * g + j] = ht
+        def copy_x(q, a, copy):
+            if a == 0:
+                xg_of[q] = xg_pool.tile([P, 2048], BF16, name="xg", align_bytes=64)
+            copy(
+                out=xg_of[q][:, 1024 * a : 1024 * (a + 1)].bitcast(F32).rearrange("p (c r u) -> p c r u", c=2, u=2),
+                in_=xt_of[(q, a)][:].rearrange("p (c u r) -> p c r u", c=2, u=2),
+            )
+
+        def quantise_x(q):
+            cod = xc_pool.tile([P, 512], U32, name="x_cod", align_bytes=64)
+            scl = xc_pool.tile([P, 512], U8, name="x_scl", align_bytes=64)
+            nc.vector.quantize_mx(out=cod[:].bitcast(FP8X4), scales=scl[:], in_=xg_of[q][:])
+            xc_of[q] = (cod, scl)
+
+        def stage1(q):
+            cod, scl = xc_of[q]
+            for a in range(2):
+                ht = ht_pool.tile([P, 512], F32, name="ht")
+                ht_of[(q, a)] = ht
                 for t in range(4):
                     for c in range(2):
                         wcols = slice(512 * c + P * t, 512 * c + P * (t + 1))
-                        xcols = slice(256 * j + P * c, 256 * j + P * (c + 1))
+                        xcols = slice(256 * a + P * c, 256 * a + P * (c + 1))
                         nc.tensor.matmul_mx(
                             out=ht[:, P * t : P * (t + 1)],
                             lhsT=p_cod[:, wcols].bitcast(FP8X4),
@@ -175,33 +154,33 @@ def tile_adaptiveinputsoftmax_pa_t_kernel(tc, x, tail_proj_0, tail_w_0, cluster_
                             stop=(c == 1),
                         )
 
-        def copy_h(g):
-            hg = hg_pool.tile([P, 2048], BF16, name="hg", align_bytes=64)
-            hg_of[g] = hg
-            for j in range(4):
-                copy = nc.scalar.copy if (j < S_HC or g == QUADS - 1) else nc.vector.tensor_copy
-                copy(
-                    out=hg[:, 512 * j : 512 * (j + 1)].rearrange("p (r t) -> p r t", t=4),
-                    in_=ht_of[4 * g + j][:].rearrange("p (t r) -> p r t", t=4),
-                )
+        def copy_h(q, a, copy):
+            if q not in hg_of:
+                hg_of[q] = hg_pool.tile([P, 1024], BF16, name="hg", align_bytes=64)
+            copy(
+                out=hg_of[q][:, 512 * a : 512 * (a + 1)].rearrange("p (r t) -> p r t", t=4),
+                in_=ht_of[(q, a)][:].rearrange("p (t r) -> p r t", t=4),
+            )
 
-        def quantise_h(g):
-            cols = slice(512 * g, 512 * (g + 1))
-            nc.vector.quantize_mx(out=h_cod[:, cols].bitcast(FP8X4), scales=h_scl[:, cols], in_=hg_of[g][:])
+        def quantise_h(q):
+            cols = slice(256 * q, 256 * (q + 1))
+            nc.vector.quantize_mx(out=h_cod[:, cols].bitcast(FP8X4), scales=h_scl[:, cols], in_=hg_of[q][:])
 
-        def stage2(i):
-            for v in range(2):
-                lg = ps_pool.tile([P, 512], F32, name="bank")
-                nc.tensor.matmul_mx(
-                    out=lg[:],
-                    lhsT=h_cod[:, P * i : P * (i + 1)].bitcast(FP8X4),
-                    lhsT_scale=h_scl[:, P * i : P * (i + 1)],
-                    rhs=w_cod[:, 512 * v : 512 * (v + 1)].bitcast(FP8X4),
-                    rhs_scale=w_scl[:, 512 * v : 512 * (v + 1)],
-                    start=True,
-                    stop=True,
-                )
-                lg_of[(i, v)] = lg
+        def stage2(q):
+            for a in range(2):
+                i = 2 * q + a
+                for v in range(2):
+                    lg = lg_pool.tile([P, 512], F32, name="lg")
+                    nc.tensor.matmul_mx(
+                        out=lg[:],
+                        lhsT=h_cod[:, P * i : P * (i + 1)].bitcast(FP8X4),
+                        lhsT_scale=h_scl[:, P * i : P * (i + 1)],
+                        rhs=w_cod[:, 512 * v : 512 * (v + 1)].bitcast(FP8X4),
+                        rhs_scale=w_scl[:, 512 * v : 512 * (v + 1)],
+                        start=True,
+                        stop=True,
+                    )
+                    lg_of[(i, v)] = lg
 
         def row_max(i):
             mx = st_pool.tile([P, 4], F32, name="mx")
@@ -213,12 +192,8 @@ def tile_adaptiveinputsoftmax_pa_t_kernel(tc, x, tail_proj_0, tail_w_0, cluster_
         def exponent(i):
             q, a = divmod(i, 2)
             if a == 0:
-                e = e_pool.tile([P, 2048], F32, name="e")
-                sm = st_pool.tile([P, 4], F32, name="sm")
-                rc = st_pool.tile([P, 4], F32, name="rc")
-                e_of[q] = e
-                sm_of[q] = sm
-                rc_of[q] = rc
+                e_of[q] = e_pool.tile([P, 2048], F32, name="e")
+                sm_of[q] = st_pool.tile([P, 4], F32, name="sm")
             for v in range(2):
                 first = 1024 * a + 512 * v
                 nc.scalar.activation(
@@ -231,63 +206,69 @@ def tile_adaptiveinputsoftmax_pa_t_kernel(tc, x, tail_proj_0, tail_w_0, cluster_
                 )
 
         def finish(q, halves, engine):
-            lo, n = halves[0], len(halves)
-            sm = sm_of[q]
-            rc = rc_of[q]
+            n = len(halves)
+            rc = st_pool.tile([P, 4], F32, name="rc")
             nc.vector.tensor_reduce(
-                out=rc[:, lo : lo + n],
-                in_=sm[:, 2 * lo : 2 * (lo + n)].rearrange("p (a v) -> p a v", v=2),
+                out=rc[:, 0:n],
+                in_=sm_of[q][:, 2 * halves[0] : 2 * (halves[0] + n)].rearrange("p (a v) -> p a v", v=2),
                 axis=AX.X,
                 op=ALU.add,
             )
-            nc.vector.reciprocal(out=rc[:, 2 + lo : 2 + lo + n], in_=rc[:, lo : lo + n])
-            for a in halves:
+            nc.vector.reciprocal(out=rc[:, 2 : 2 + n], in_=rc[:, 0:n])
+            for k, a in enumerate(halves):
                 i = 2 * q + a
                 part = e_of[q][:, 1024 * a : 1024 * (a + 1)]
                 engine.tensor_scalar(
                     out=part,
                     in0=part,
-                    scalar1=rc[:, 2 + a : 3 + a],
+                    scalar1=rc[:, 2 + k : 3 + k],
                     scalar2=prob[:, i : i + 1],
                     op0=ALU.mult,
                     op1=ALU.mult,
                 )
                 nc.sync.dma_start(out=out_rows[:, 1024 * i : 1024 * (i + 1)], in_=part)
 
-        def back_end(i):
-            if i < TILES:
-                stage2(i)
-                row_max(i)
-                exponent(i)
-            if i == EARLY + 1:
-                quantise_h(QUADS - 1)
-            d = i - DELAY
-            if d >= 0 and d % 2 == 1 and d < TILES - TAIL:
-                finish(d // 2, [0, 1], nc.gpsimd)
-            if d == TILES - TAIL and d % 2 == 0 and GTAIL:
-                finish(d // 2, [0], nc.gpsimd)
+        def has(q):
+            return 0 <= q < PAIRS
 
-        prepare_proj()
-        transposes(0)
-        copy_x(0)
-        quantise_x(0)
-        for g in range(QUADS):
-            if g + 1 < QUADS:
-                transposes(g + 1)
-            else:
-                for i in range(EARLY):
-                    back_end(i)
-            stage1(g)
-            if g + 1 < QUADS:
-                copy_x(g + 1)
-                quantise_x(g + 1)
-            if g == 1:
-                prepare_w()
-            copy_h(g)
-            if g + 1 < QUADS:
-                quantise_h(g)
-        for i in range(EARLY, TILES + DELAY):
-            back_end(i)
-            if i == TILES - 1:
-                for d in range(TILES - TAIL + GTAIL, TILES):
-                    finish(d // 2, [d % 2], nc.vector)
+        group_proj(0, nc.vector.tensor_copy, (0, 4))
+        group_proj(1, nc.vector.tensor_copy, (0, 2))
+        group_proj(1, nc.scalar.copy, (2, 4))
+        quantise_proj(0)
+        quantise_proj(1)
+        for n in range(-4, PAIRS + 1):
+            if has(n):
+                stage2(n)
+            if has(n + 1):
+                copy_h(n + 1, 0, nc.scalar.copy)
+            if has(n + 3):
+                copy_x(n + 3, 0, nc.scalar.copy)
+                copy_x(n + 3, 1, nc.scalar.copy)
+            if has(n + 4):
+                transposes(n + 4)
+            if has(n + 2):
+                stage1(n + 2)
+            if n == -2:
+                group_w(1, nc.scalar.copy)
+            if has(n):
+                for i in (2 * n, 2 * n + 1):
+                    row_max(i)
+                    exponent(i)
+            if has(n + 3):
+                quantise_x(n + 3)
+            if n == -2:
+                group_w(0, nc.vector.tensor_copy)
+                quantise_w(0)
+            if n == -1:
+                quantise_w(1)
+                nc.vector.tensor_copy(out=prob[:], in_=prob_bf[:])
+            if has(n + 1):
+                quantise_h(n + 1)
+            if has(n - 1):
+                if n - 1 < PAIRS - 1:
+                    finish(n - 1, [0, 1], nc.gpsimd)
+                else:
+                    finish(n - 1, [0], nc.vector)
+                    finish(n - 1, [1], nc.vector)
+            if has(n + 2):
+                copy_h(n + 2, 1, nc.vector.tensor_copy)

@@ -111,6 +111,7 @@ def tile_adaptiveinputsoftmax_pa_t_kernel(tc, x, tail_proj_0, tail_w_0, cluster_
         mx_of = {}
         e_of = {}
         sm_of = {}
+        rc_of = {}
 
         def transposes(q):
             words = x_sb[q][:].bitcast(F32)
@@ -182,11 +183,13 @@ def tile_adaptiveinputsoftmax_pa_t_kernel(tc, x, tail_proj_0, tail_w_0, cluster_
                     )
                     lg_of[(i, v)] = lg
 
-        def row_max(i):
-            mx = st_pool.tile([P, 4], F32, name="mx")
-            mx_of[i] = mx
-            for v in range(2):
-                nc.vector.tensor_reduce(out=mx[:, v : v + 1], in_=lg_of[(i, v)][:], axis=AX.X, op=ALU.max)
+        def bank_max(i, v):
+            if v == 0:
+                mx_of[i] = st_pool.tile([P, 4], F32, name="mx")
+            nc.vector.tensor_reduce(out=mx_of[i][:, v : v + 1], in_=lg_of[(i, v)][:], axis=AX.X, op=ALU.max)
+
+        def join_max(i):
+            mx = mx_of[i]
             nc.vector.tensor_reduce(out=mx[:, 2:3], in_=mx[:, 0:2], axis=AX.X, op=ALU.max, negate=True)
 
         def exponent(i):
@@ -205,23 +208,28 @@ def tile_adaptiveinputsoftmax_pa_t_kernel(tc, x, tail_proj_0, tail_w_0, cluster_
                     accum_out=sm_of[q][:, 2 * a + v : 2 * a + v + 1],
                 )
 
-        def finish(q, halves, engine):
+        def row_sum(q, halves):
             n = len(halves)
-            rc = st_pool.tile([P, 4], F32, name="rc")
+            if q not in rc_of:
+                rc_of[q] = st_pool.tile([P, 4], F32, name="rc")
             nc.vector.tensor_reduce(
-                out=rc[:, 0:n],
+                out=rc_of[q][:, halves[0] : halves[0] + n],
                 in_=sm_of[q][:, 2 * halves[0] : 2 * (halves[0] + n)].rearrange("p (a v) -> p a v", v=2),
                 axis=AX.X,
                 op=ALU.add,
             )
-            nc.vector.reciprocal(out=rc[:, 2 : 2 + n], in_=rc[:, 0:n])
-            for k, a in enumerate(halves):
+
+        def scale(q, halves, engine):
+            lo, n = halves[0], len(halves)
+            rc = rc_of[q]
+            nc.vector.reciprocal(out=rc[:, 2 + lo : 2 + lo + n], in_=rc[:, lo : lo + n])
+            for a in halves:
                 i = 2 * q + a
                 part = e_of[q][:, 1024 * a : 1024 * (a + 1)]
                 engine.tensor_scalar(
                     out=part,
                     in0=part,
-                    scalar1=rc[:, 2 + k : 3 + k],
+                    scalar1=rc[:, 2 + a : 3 + a],
                     scalar2=prob[:, i : i + 1],
                     op0=ALU.mult,
                     op1=ALU.mult,
@@ -236,7 +244,7 @@ def tile_adaptiveinputsoftmax_pa_t_kernel(tc, x, tail_proj_0, tail_w_0, cluster_
         group_proj(1, nc.scalar.copy, (2, 4))
         quantise_proj(0)
         quantise_proj(1)
-        for n in range(-4, PAIRS + 1):
+        for n in range(-4, PAIRS):
             if has(n):
                 stage2(n)
             if has(n + 1):
@@ -251,11 +259,19 @@ def tile_adaptiveinputsoftmax_pa_t_kernel(tc, x, tail_proj_0, tail_w_0, cluster_
             if n == -2:
                 group_w(1, nc.scalar.copy)
             if has(n):
-                for i in (2 * n, 2 * n + 1):
-                    row_max(i)
-                    exponent(i)
+                bank_max(2 * n, 0)
+                bank_max(2 * n, 1)
+                bank_max(2 * n + 1, 0)
+                join_max(2 * n)
+                bank_max(2 * n + 1, 1)
+                exponent(2 * n)
+            if has(n - 1):
+                row_sum(n - 1, [0, 1])
             if has(n + 3):
                 quantise_x(n + 3)
+            if has(n):
+                join_max(2 * n + 1)
+                exponent(2 * n + 1)
             if n == -2:
                 group_w(0, nc.vector.tensor_copy)
                 quantise_w(0)
@@ -265,10 +281,9 @@ def tile_adaptiveinputsoftmax_pa_t_kernel(tc, x, tail_proj_0, tail_w_0, cluster_
             if has(n + 1):
                 quantise_h(n + 1)
             if has(n - 1):
-                if n - 1 < PAIRS - 1:
-                    finish(n - 1, [0, 1], nc.gpsimd)
-                else:
-                    finish(n - 1, [0], nc.vector)
-                    finish(n - 1, [1], nc.vector)
+                scale(n - 1, [0, 1], nc.gpsimd)
             if has(n + 2):
                 copy_h(n + 2, 1, nc.vector.tensor_copy)
+        for a in range(2):
+            row_sum(PAIRS - 1, [a])
+            scale(PAIRS - 1, [a], nc.vector)

@@ -55,16 +55,26 @@ def tile_adaptiveinputsoftmax_pa_t_kernel(tc, x, tail_proj_0, tail_w_0, cluster_
         h_scl = const.tile([P, TOKENS], U8, name="h_scl", align_bytes=64)
         x_sb = [const.tile([P, 2048], BF16, name="x_sb%d" % g) for g in range(PAIRS)]
 
-        for c in range(2):
+        def load_proj(c):
             nc.sync.dma_start(
                 out=p_raw[:, 2048 * c : 2048 * (c + 1)],
                 in_=tail_proj_0[512 * c : 512 * (c + 1), :].rearrange("(p j) n -> p (j n)", j=4),
             )
-        for g in range(PAIRS):
-            nc.sync.dma_start(out=x_sb[g][:], in_=x_rows[:, 2048 * g : 2048 * (g + 1)])
-            if g == 2:
-                nc.sync.dma_start(out=w_raw[:], in_=tail_w_0.rearrange("(p j) n -> p (j n)", j=4))
-                nc.sync.dma_start(out=prob_bf[:], in_=prob_rows)
+
+        def load_x(q):
+            nc.sync.dma_start(out=x_sb[q][:], in_=x_rows[:, 2048 * q : 2048 * (q + 1)])
+
+        def load_w():
+            nc.sync.dma_start(out=w_raw[:], in_=tail_w_0.rearrange("(p j) n -> p (j n)", j=4))
+            nc.sync.dma_start(out=prob_bf[:], in_=prob_rows)
+
+        load_proj(0)
+        load_x(0)
+        load_proj(1)
+        load_w()
+        load_x(1)
+        for q in range(2, PAIRS):
+            load_x(q)
 
         ident = const.tile([P, P], F32, name="ident")
         make_identity(nc, ident[:])
@@ -219,71 +229,93 @@ def tile_adaptiveinputsoftmax_pa_t_kernel(tc, x, tail_proj_0, tail_w_0, cluster_
                 op=ALU.add,
             )
 
-        def scale(q, halves, engine):
+        def invert(q, halves):
             lo, n = halves[0], len(halves)
             rc = rc_of[q]
             nc.vector.reciprocal(out=rc[:, 2 + lo : 2 + lo + n], in_=rc[:, lo : lo + n])
-            for a in halves:
-                i = 2 * q + a
-                part = e_of[q][:, 1024 * a : 1024 * (a + 1)]
-                engine.tensor_scalar(
-                    out=part,
-                    in0=part,
-                    scalar1=rc[:, 2 + a : 3 + a],
-                    scalar2=prob[:, i : i + 1],
-                    op0=ALU.mult,
-                    op1=ALU.mult,
-                )
-                nc.sync.dma_start(out=out_rows[:, 1024 * i : 1024 * (i + 1)], in_=part)
+
+        def scale(q, a, engine):
+            i = 2 * q + a
+            part = e_of[q][:, 1024 * a : 1024 * (a + 1)]
+            engine.tensor_scalar(
+                out=part,
+                in0=part,
+                scalar1=rc_of[q][:, 2 + a : 3 + a],
+                scalar2=prob[:, i : i + 1],
+                op0=ALU.mult,
+                op1=ALU.mult,
+            )
+            nc.sync.dma_start(out=out_rows[:, 1024 * i : 1024 * (i + 1)], in_=part)
 
         def has(q):
             return 0 <= q < PAIRS
 
         group_proj(0, nc.vector.tensor_copy, (0, 4))
-        group_proj(1, nc.vector.tensor_copy, (0, 2))
-        group_proj(1, nc.scalar.copy, (2, 4))
+        transposes(0)
+        copy_x(0, 0, nc.scalar.copy)
+        copy_x(0, 1, nc.scalar.copy)
         quantise_proj(0)
+        group_proj(1, nc.vector.tensor_copy, (0, 4))
+        quantise_x(0)
         quantise_proj(1)
-        for n in range(-4, PAIRS):
-            if has(n):
-                stage2(n)
+        stage1(0)
+        transposes(1)
+        group_w(1, nc.scalar.copy)
+        group_w(0, nc.vector.tensor_copy)
+        copy_h(0, 0, nc.vector.tensor_copy)
+        copy_h(0, 1, nc.scalar.copy)
+        quantise_w(0)
+        quantise_h(0)
+        copy_x(1, 0, nc.scalar.copy)
+        copy_x(1, 1, nc.scalar.copy)
+        transposes(2)
+        quantise_w(1)
+        quantise_x(1)
+        stage1(1)
+        nc.vector.tensor_copy(out=prob[:], in_=prob_bf[:])
+        copy_x(2, 0, nc.scalar.copy)
+        copy_x(2, 1, nc.scalar.copy)
+        transposes(3)
+        copy_h(1, 0, nc.vector.tensor_copy)
+        quantise_x(2)
+        for n in range(0, PAIRS):
+            stage2(n)
             if has(n + 1):
-                copy_h(n + 1, 0, nc.scalar.copy)
+                copy_h(n + 1, 1, nc.scalar.copy)
+            if has(n + 2):
+                stage1(n + 2)
             if has(n + 3):
                 copy_x(n + 3, 0, nc.scalar.copy)
                 copy_x(n + 3, 1, nc.scalar.copy)
             if has(n + 4):
                 transposes(n + 4)
-            if has(n + 2):
-                stage1(n + 2)
-            if n == -2:
-                group_w(1, nc.scalar.copy)
-            if has(n):
-                bank_max(2 * n, 0)
-                bank_max(2 * n, 1)
-                bank_max(2 * n + 1, 0)
-                join_max(2 * n)
-                bank_max(2 * n + 1, 1)
-                exponent(2 * n)
-            if has(n - 1):
+            bank_max(2 * n, 0)
+            bank_max(2 * n, 1)
+            if not has(n + 1):
                 row_sum(n - 1, [0, 1])
-            if has(n + 3):
-                quantise_x(n + 3)
-            if has(n):
-                join_max(2 * n + 1)
-                exponent(2 * n + 1)
-            if n == -2:
-                group_w(0, nc.vector.tensor_copy)
-                quantise_w(0)
-            if n == -1:
-                quantise_w(1)
-                nc.vector.tensor_copy(out=prob[:], in_=prob_bf[:])
+            bank_max(2 * n + 1, 0)
+            join_max(2 * n)
+            if not has(n + 1):
+                invert(n - 1, [0, 1])
+                scale(n - 1, 0, nc.gpsimd)
+            bank_max(2 * n + 1, 1)
+            exponent(2 * n)
+            if has(n - 1) and has(n + 1):
+                row_sum(n - 1, [0, 1])
             if has(n + 1):
                 quantise_h(n + 1)
-            if has(n - 1):
-                scale(n - 1, [0, 1], nc.gpsimd)
+            join_max(2 * n + 1)
+            exponent(2 * n + 1)
+            if has(n + 3):
+                quantise_x(n + 3)
+            if has(n - 1) and has(n + 1):
+                invert(n - 1, [0, 1])
+                scale(n - 1, 0, nc.gpsimd)
+                scale(n - 1, 1, nc.gpsimd)
             if has(n + 2):
-                copy_h(n + 2, 1, nc.vector.tensor_copy)
+                copy_h(n + 2, 0, nc.vector.tensor_copy)
+        scale(PAIRS - 2, 1, nc.vector)
         for a in range(2):
             row_sum(PAIRS - 1, [a])
-            scale(PAIRS - 1, [a], nc.vector)
+            invert(PAIRS - 1, [a])
+            scale(PAIRS - 1, a, nc.vector)

@@ -71,8 +71,8 @@ def tile_adaptiveinputsoftmax_pa_t_kernel(tc, x, tail_proj_0, tail_w_0, cluster_
         load_proj(0)
         load_x(0)
         load_proj(1)
-        load_w()
         load_x(1)
+        load_w()
         for q in range(2, PAIRS):
             load_x(q)
 
@@ -98,11 +98,11 @@ def tile_adaptiveinputsoftmax_pa_t_kernel(tc, x, tail_proj_0, tail_w_0, cluster_
                 in_=p_grp[:, 2048 * c : 2048 * (c + 1)],
             )
 
-        def group_w(v, copy):
+        def group_w(lo, hi, copy):
             rows = w_raw[:].rearrange("p (j n) -> p j n", j=4)
             copy(
-                out=w_grp[:, 2048 * v : 2048 * (v + 1)].rearrange("p (a i j) -> p a j i", i=4, j=4),
-                in_=rows[:, :, 512 * v : 512 * (v + 1)].rearrange("p j (a i) -> p a j i", i=4),
+                out=w_grp[:, 4 * lo : 4 * hi].rearrange("p (a i j) -> p a j i", i=4, j=4),
+                in_=rows[:, :, lo:hi].rearrange("p j (a i) -> p a j i", i=4),
             )
 
         def quantise_w(v):
@@ -126,7 +126,10 @@ def tile_adaptiveinputsoftmax_pa_t_kernel(tc, x, tail_proj_0, tail_w_0, cluster_
         def transposes(q):
             words = x_sb[q][:].bitcast(F32)
             for a in range(2):
-                xt = xt_pool.tile([P, 512], F32, name="xt")
+                if q == 1:
+                    xt = lg_pool.tile([P, 512], F32, name="lg")
+                else:
+                    xt = xt_pool.tile([P, 512], F32, name="xt")
                 for s in range(4):
                     first = 512 * a + 256 * (s // 2) + s % 2
                     nc.tensor.transpose(xt[:, P * s : P * (s + 1)], words[:, first : first + 255 : 2], ident[:])
@@ -149,7 +152,10 @@ def tile_adaptiveinputsoftmax_pa_t_kernel(tc, x, tail_proj_0, tail_w_0, cluster_
         def stage1(q):
             cod, scl = xc_of[q]
             for a in range(2):
-                ht = ht_pool.tile([P, 512], F32, name="ht")
+                if q == 1:
+                    ht = lg_pool.tile([P, 512], F32, name="lg")
+                else:
+                    ht = ht_pool.tile([P, 512], F32, name="ht")
                 ht_of[(q, a)] = ht
                 for t in range(4):
                     for c in range(2):
@@ -252,35 +258,38 @@ def tile_adaptiveinputsoftmax_pa_t_kernel(tc, x, tail_proj_0, tail_w_0, cluster_
 
         group_proj(0, nc.vector.tensor_copy, (0, 4))
         transposes(0)
+        transposes(1)
         copy_x(0, 0, nc.scalar.copy)
         copy_x(0, 1, nc.scalar.copy)
         quantise_proj(0)
         group_proj(1, nc.vector.tensor_copy, (0, 4))
         quantise_x(0)
         quantise_proj(1)
-        stage1(0)
-        transposes(1)
-        group_w(1, nc.scalar.copy)
-        group_w(0, nc.vector.tensor_copy)
-        copy_h(0, 0, nc.vector.tensor_copy)
-        copy_h(0, 1, nc.scalar.copy)
-        quantise_w(0)
-        quantise_h(0)
         copy_x(1, 0, nc.scalar.copy)
         copy_x(1, 1, nc.scalar.copy)
-        transposes(2)
-        quantise_w(1)
+        stage1(0)
         quantise_x(1)
         stage1(1)
-        nc.vector.tensor_copy(out=prob[:], in_=prob_bf[:])
+        transposes(2)
+        group_w(0, 512, nc.vector.tensor_copy)
+        group_w(768, 1024, nc.scalar.copy)
+        copy_h(0, 0, nc.scalar.copy)
+        copy_h(0, 1, nc.scalar.copy)
+        group_w(512, 768, nc.vector.tensor_copy)
+        copy_h(1, 0, nc.scalar.copy)
+        copy_h(1, 1, nc.scalar.copy)
+        quantise_w(0)
+        quantise_h(0)
+        quantise_w(1)
         copy_x(2, 0, nc.scalar.copy)
         copy_x(2, 1, nc.scalar.copy)
-        transposes(3)
-        copy_h(1, 0, nc.vector.tensor_copy)
+        nc.vector.tensor_copy(out=prob[:], in_=prob_bf[:])
         quantise_x(2)
         for n in range(0, PAIRS):
             stage2(n)
-            if has(n + 1):
+            if n == 0:
+                transposes(3)
+            elif has(n + 1):
                 copy_h(n + 1, 1, nc.scalar.copy)
             if has(n + 2):
                 stage1(n + 2)

@@ -82,6 +82,14 @@ def tile_adaptiveinputsoftmax_pa_t_kernel(tc, x, tail_proj_0, tail_w_0, cluster_
         warm_out = const.tile([P, 1], F32, name="warm_out")
         nc.vector.memset(warm_in[:], 0.0)
         nc.scalar.activation(out=warm_out[:], in_=warm_in[:], func=ACT.Exp)
+        idle_in = const.tile([P, 512], BF16, name="idle_in")
+        nc.vector.memset(idle_in[:], 0.0)
+
+        def keep_clock(count):
+            for k in range(count):
+                idle_out = ht_pool.tile([P, 512], F32, name="ht")
+                nc.tensor.matmul(out=idle_out[:], lhsT=idle_in[:, 0:P], rhs=idle_in[:], start=True, stop=True)
+
 
         def group_proj(c, copy, slots):
             cols = slice(2048 * c, 2048 * (c + 1))
@@ -257,8 +265,11 @@ def tile_adaptiveinputsoftmax_pa_t_kernel(tc, x, tail_proj_0, tail_w_0, cluster_
             return 0 <= q < PAIRS
 
         group_proj(0, nc.vector.tensor_copy, (0, 4))
+        keep_clock(6)
         transposes(0)
+        keep_clock(3)
         transposes(1)
+        keep_clock(2)
         copy_x(0, 0, nc.scalar.copy)
         copy_x(0, 1, nc.scalar.copy)
         quantise_proj(0)

@@ -326,10 +326,11 @@ def tile_adaptiveinputsoftmax_pa_t_kernel(tc, x, tail_proj_0, tail_w_0, cluster_
                 quantise_h(n + 1)
             join_max(2 * n + 1)
             exponent(2 * n + 1)
+            if has(n - 1) and has(n + 1):
+                invert(n - 1, [0, 1])
             if has(n + 3):
                 quantise_x(n + 3)
             if has(n - 1) and has(n + 1):
-                invert(n - 1, [0, 1])
                 scale(n - 1, 0, nc.gpsimd)
                 scale(n - 1, 1, nc.gpsimd)
             if has(n + 2):

@@ -85,9 +85,12 @@ def tile_adaptiveinputsoftmax_pa_t_kernel(tc, x, tail_proj_0, tail_w_0, cluster_
         idle_in = const.tile([P, 512], BF16, name="idle_in")
         nc.vector.memset(idle_in[:], 0.0)
 
-        def keep_clock(count):
+        def keep_clock(count, late=False):
             for k in range(count):
-                idle_out = ht_pool.tile([P, 512], F32, name="ht")
+                if late:
+                    idle_out = xt_pool.tile([P, 512], F32, name="xt")
+                else:
+                    idle_out = ht_pool.tile([P, 512], F32, name="ht")
                 nc.tensor.matmul(out=idle_out[:], lhsT=idle_in[:, 0:P], rhs=idle_in[:], start=True, stop=True)
 
 
@@ -248,18 +251,21 @@ def tile_adaptiveinputsoftmax_pa_t_kernel(tc, x, tail_proj_0, tail_w_0, cluster_
             rc = rc_of[q]
             nc.vector.reciprocal(out=rc[:, 2 + lo : 2 + lo + n], in_=rc[:, lo : lo + n])
 
-        def scale(q, a, engine):
+        def scale(q, a, engine, parts=1):
             i = 2 * q + a
-            part = e_of[q][:, 1024 * a : 1024 * (a + 1)]
-            engine.tensor_scalar(
-                out=part,
-                in0=part,
-                scalar1=rc_of[q][:, 2 + a : 3 + a],
-                scalar2=prob[:, i : i + 1],
-                op0=ALU.mult,
-                op1=ALU.mult,
-            )
-            nc.sync.dma_start(out=out_rows[:, 1024 * i : 1024 * (i + 1)], in_=part)
+            width = V0 // parts
+            for k in range(parts):
+                part = e_of[q][:, 1024 * a + width * k : 1024 * a + width * (k + 1)]
+                engine.tensor_scalar(
+                    out=part,
+                    in0=part,
+                    scalar1=rc_of[q][:, 2 + a : 3 + a],
+                    scalar2=prob[:, i : i + 1],
+                    op0=ALU.mult,
+                    op1=ALU.mult,
+                )
+                first = 1024 * i + width * k
+                nc.sync.dma_start(out=out_rows[:, first : first + width], in_=part)
 
         def has(q):
             return 0 <= q < PAIRS
@@ -298,6 +304,8 @@ def tile_adaptiveinputsoftmax_pa_t_kernel(tc, x, tail_proj_0, tail_w_0, cluster_
         quantise_x(2)
         for n in range(0, PAIRS):
             stage2(n)
+            if n == PAIRS - 2:
+                keep_clock(4, late=True)
             if n == 0:
                 transposes(3)
             elif has(n + 1):
@@ -339,4 +347,4 @@ def tile_adaptiveinputsoftmax_pa_t_kernel(tc, x, tail_proj_0, tail_w_0, cluster_
         for a in range(2):
             row_sum(PAIRS - 1, [a])
             invert(PAIRS - 1, [a])
-            scale(PAIRS - 1, a, nc.vector)
+            scale(PAIRS - 1, a, nc.vector, 2)

from contextlib import ExitStack

import concourse.mybir as mybir
from concourse.masks import make_identity

F32 = mybir.dt.float32
BF16 = mybir.dt.bfloat16
U32 = mybir.dt.uint32
U8 = mybir.dt.uint8
FP8X4 = mybir.dt.float8_e4m3fn_x4
ALU = mybir.AluOpType
ACT = mybir.ActivationFunctionType
AX = mybir.AxisListType

P = 128
TOKENS = 4096
H = 1024
P0 = 512
V0 = 1024
TILES = TOKENS // P
PAIRS = TILES // 2

FLOPS = 2 * TOKENS * H * P0 + 2 * TOKENS * P0 * V0


def tile_adaptiveinputsoftmax_pa_t_kernel(tc, x, tail_proj_0, tail_w_0, cluster_prob, out):
    nc = tc.nc
    with ExitStack() as ctx:
        const = ctx.enter_context(tc.tile_pool(name="const", bufs=1))
        xg_pool = ctx.enter_context(tc.tile_pool(name="xg_pool", bufs=3))
        xc_pool = ctx.enter_context(tc.tile_pool(name="xc_pool", bufs=3))
        hg_pool = ctx.enter_context(tc.tile_pool(name="hg_pool", bufs=3))
        e_pool = ctx.enter_context(tc.tile_pool(name="e_pool", bufs=5))
        st_pool = ctx.enter_context(tc.tile_pool(name="st_pool", bufs=8))
        xt_pool = ctx.enter_context(tc.psum_pool(name="xt_pool", bufs=2))
        ht_pool = ctx.enter_context(tc.psum_pool(name="ht_pool", bufs=2))
        lg_pool = ctx.enter_context(tc.psum_pool(name="lg_pool", bufs=4))
        ctx.enter_context(tc.manual_schedule())

        x_rows = x.flatten_outer_dims().rearrange("(p i) k -> p (i k)", i=TILES)
        out_rows = out.flatten_outer_dims().rearrange("(p i) v -> p (i v)", i=TILES)
        prob_rows = cluster_prob.rearrange("n t o -> (n t o)").rearrange("(p i) -> p i", i=TILES)

        p_raw = const.tile([P, 4096], BF16, name="p_raw")
        p_grp = const.tile([P, 4096], BF16, name="p_grp", align_bytes=64)
        p_cod = const.tile([P, 1024], U32, name="p_cod", align_bytes=64)
        p_scl = const.tile([P, 1024], U8, name="p_scl", align_bytes=64)
        w_raw = const.tile([P, 4096], BF16, name="w_raw")
        w_grp = const.tile([P, 4096], BF16, name="w_grp", align_bytes=64)
        w_cod = const.tile([P, 1024], U32, name="w_cod", align_bytes=64)
        w_scl = const.tile([P, 1024], U8, name="w_scl", align_bytes=64)
        prob_bf = const.tile([P, TILES], BF16, name="prob_bf")
        prob = const.tile([P, TILES], F32, name="prob")
        h_cod = const.tile([P, TOKENS], U32, name="h_cod", align_bytes=64)
        h_scl = const.tile([P, TOKENS], U8, name="h_scl", align_bytes=64)
        x_sb = [const.tile([P, 2048], BF16, name="x_sb%d" % g) for g in range(PAIRS)]

        def load_proj(c):
            nc.sync.dma_start(
                out=p_raw[:, 2048 * c : 2048 * (c + 1)],
                in_=tail_proj_0[512 * c : 512 * (c + 1), :].rearrange("(p j) n -> p (j n)", j=4),
            )

        def load_x(q):
            nc.sync.dma_start(out=x_sb[q][:], in_=x_rows[:, 2048 * q : 2048 * (q + 1)])

        def load_w():
            nc.sync.dma_start(out=w_raw[:], in_=tail_w_0.rearrange("(p j) n -> p (j n)", j=4))
            nc.sync.dma_start(out=prob_bf[:], in_=prob_rows)

        load_proj(0)
        load_x(0)
        load_proj(1)
        load_x(1)
        load_w()
        for q in range(2, PAIRS):
            load_x(q)

        ident = const.tile([P, P], F32, name="ident")
        make_identity(nc, ident[:])
        warm_in = const.tile([P, 1], F32, name="warm_in")
        warm_out = const.tile([P, 1], F32, name="warm_out")
        nc.vector.memset(warm_in[:], 0.0)
        nc.scalar.activation(out=warm_out[:], in_=warm_in[:], func=ACT.Exp)
        idle_in = const.tile([P, 512], BF16, name="idle_in")
        nc.vector.memset(idle_in[:], 0.0)

        def keep_clock(count, late=False):
            for k in range(count):
                if late:
                    idle_out = xt_pool.tile([P, 512], F32, name="xt")
                else:
                    idle_out = ht_pool.tile([P, 512], F32, name="ht")
                nc.tensor.matmul(out=idle_out[:], lhsT=idle_in[:, 0:P], rhs=idle_in[:], start=True, stop=True)


        def group_proj(c, copy, slots):
            cols = slice(2048 * c, 2048 * (c + 1))
            lo, hi = slots
            copy(
                out=p_grp[:, cols].rearrange("p (t m j) -> p t m j", t=4, j=4)[:, lo:hi],
                in_=p_raw[:, cols].rearrange("p (j m t) -> p t m j", j=4, t=4)[:, lo:hi],
            )

        def quantise_proj(c):
            nc.vector.quantize_mx(
                out=p_cod[:, 512 * c : 512 * (c + 1)].bitcast(FP8X4),
                scales=p_scl[:, 512 * c : 512 * (c + 1)],
                in_=p_grp[:, 2048 * c : 2048 * (c + 1)],
            )

        def group_w(lo, hi, copy):
            rows = w_raw[:].rearrange("p (j n) -> p j n", j=4)
            copy(
                out=w_grp[:, 4 * lo : 4 * hi].rearrange("p (a i j) -> p a j i", i=4, j=4),
                in_=rows[:, :, lo:hi].rearrange("p j (a i) -> p a j i", i=4),
            )

        def quantise_w(v):
            nc.vector.quantize_mx(
                out=w_cod[:, 512 * v : 512 * (v + 1)].bitcast(FP8X4),
                scales=w_scl[:, 512 * v : 512 * (v + 1)],
                in_=w_grp[:, 2048 * v : 2048 * (v + 1)],
            )

        xt_of = {}
        xg_of = {}
        xc_of = {}
        ht_of = {}
        hg_of = {}
        lg_of = {}
        mx_of = {}
        e_of = {}
        sm_of = {}
        rc_of = {}

        def transposes(q):
            words = x_sb[q][:].bitcast(F32)
            for a in range(2):
                if q == 1:
                    xt = lg_pool.tile([P, 512], F32, name="lg")
                else:
                    xt = xt_pool.tile([P, 512], F32, name="xt")
                for s in range(4):
                    first = 512 * a + 256 * (s // 2) + s % 2
                    nc.tensor.transpose(xt[:, P * s : P * (s + 1)], words[:, first : first + 255 : 2], ident[:])
                xt_of[(q, a)] = xt

        def copy_x(q, a, copy):
            if a == 0:
                xg_of[q] = xg_pool.tile([P, 2048], BF16, name="xg", align_bytes=64)
            copy(
                out=xg_of[q][:, 1024 * a : 1024 * (a + 1)].bitcast(F32).rearrange("p (c r u) -> p c r u", c=2, u=2),
                in_=xt_of[(q, a)][:].rearrange("p (c u r) -> p c r u", c=2, u=2),
            )

        def quantise_x(q):
            cod = xc_pool.tile([P, 512], U32, name="x_cod", align_bytes=64)
            scl = xc_pool.tile([P, 512], U8, name="x_scl", align_bytes=64)
            nc.vector.quantize_mx(out=cod[:].bitcast(FP8X4), scales=scl[:], in_=xg_of[q][:])
            xc_of[q] = (cod, scl)

        def stage1(q):
            cod, scl = xc_of[q]
            for a in range(2):
                if q == 1:
                    ht = lg_pool.tile([P, 512], F32, name="lg")
                else:
                    ht = ht_pool.tile([P, 512], F32, name="ht")
                ht_of[(q, a)] = ht
                for t in range(4):
                    for c in range(2):
                        wcols = slice(512 * c + P * t, 512 * c + P * (t + 1))
                        xcols = slice(256 * a + P * c, 256 * a + P * (c + 1))
                        nc.tensor.matmul_mx(
                            out=ht[:, P * t : P * (t + 1)],
                            lhsT=p_cod[:, wcols].bitcast(FP8X4),
                            lhsT_scale=p_scl[:, wcols],
                            rhs=cod[:, xcols].bitcast(FP8X4),
                            rhs_scale=scl[:, xcols],
                            start=(c == 0),
                            stop=(c == 1),
                        )

        def copy_h(q, a, copy):
            if q not in hg_of:
                hg_of[q] = hg_pool.tile([P, 1024], BF16, name="hg", align_bytes=64)
            copy(
                out=hg_of[q][:, 512 * a : 512 * (a + 1)].rearrange("p (r t) -> p r t", t=4),
                in_=ht_of[(q, a)][:].rearrange("p (t r) -> p r t", t=4),
            )

        def quantise_h(q):
            cols = slice(256 * q, 256 * (q + 1))
            nc.vector.quantize_mx(out=h_cod[:, cols].bitcast(FP8X4), scales=h_scl[:, cols], in_=hg_of[q][:])

        def stage2(q):
            for a in range(2):
                i = 2 * q + a
                for v in range(2):
                    lg = lg_pool.tile([P, 512], F32, name="lg")
                    nc.tensor.matmul_mx(
                        out=lg[:],
                        lhsT=h_cod[:, P * i : P * (i + 1)].bitcast(FP8X4),
                        lhsT_scale=h_scl[:, P * i : P * (i + 1)],
                        rhs=w_cod[:, 512 * v : 512 * (v + 1)].bitcast(FP8X4),
                        rhs_scale=w_scl[:, 512 * v : 512 * (v + 1)],
                        start=True,
                        stop=True,
                    )
                    lg_of[(i, v)] = lg

        def bank_max(i, v):
            if v == 0:
                mx_of[i] = st_pool.tile([P, 4], F32, name="mx")
            nc.vector.tensor_reduce(out=mx_of[i][:, v : v + 1], in_=lg_of[(i, v)][:], axis=AX.X, op=ALU.max)

        def join_max(i):
            mx = mx_of[i]
            nc.vector.tensor_reduce(out=mx[:, 2:3], in_=mx[:, 0:2], axis=AX.X, op=ALU.max, negate=True)

        def exponent(i):
            q, a = divmod(i, 2)
            if a == 0:
                e_of[q] = e_pool.tile([P, 2048], F32, name="e")
                sm_of[q] = st_pool.tile([P, 4], F32, name="sm")
            for v in range(2):
                first = 1024 * a + 512 * v
                nc.scalar.activation(
                    out=e_of[q][:, first : first + 512],
                    in_=lg_of[(i, v)][:],
                    func=ACT.Exp,
                    bias=mx_of[i][:, 2:3],
                    scale=1.0,
                    accum_out=sm_of[q][:, 2 * a + v : 2 * a + v + 1],
                )

        def row_sum(q, halves):
            n = len(halves)
            if q not in rc_of:
                rc_of[q] = st_pool.tile([P, 4], F32, name="rc")
            nc.vector.tensor_reduce(
                out=rc_of[q][:, halves[0] : halves[0] + n],
                in_=sm_of[q][:, 2 * halves[0] : 2 * (halves[0] + n)].rearrange("p (a v) -> p a v", v=2),
                axis=AX.X,
                op=ALU.add,
            )

        def invert(q, halves):
            lo, n = halves[0], len(halves)
            rc = rc_of[q]
            nc.vector.reciprocal(out=rc[:, 2 + lo : 2 + lo + n], in_=rc[:, lo : lo + n])

        def scale(q, a, engine, parts=1):
            i = 2 * q + a
            width = V0 // parts
            for k in range(parts):
                part = e_of[q][:, 1024 * a + width * k : 1024 * a + width * (k + 1)]
                engine.tensor_scalar(
                    out=part,
                    in0=part,
                    scalar1=rc_of[q][:, 2 + a : 3 + a],
                    scalar2=prob[:, i : i + 1],
                    op0=ALU.mult,
                    op1=ALU.mult,
                )
                first = 1024 * i + width * k
                nc.sync.dma_start(out=out_rows[:, first : first + width], in_=part)

        def has(q):
            return 0 <= q < PAIRS

        group_proj(0, nc.vector.tensor_copy, (0, 4))
        keep_clock(6)
        transposes(0)
        keep_clock(3)
        transposes(1)
        keep_clock(2)
        copy_x(0, 0, nc.scalar.copy)
        copy_x(0, 1, nc.scalar.copy)
        quantise_proj(0)
        group_proj(1, nc.vector.tensor_copy, (0, 4))
        quantise_x(0)
        quantise_proj(1)
        copy_x(1, 0, nc.scalar.copy)
        copy_x(1, 1, nc.scalar.copy)
        stage1(0)
        quantise_x(1)
        stage1(1)
        transposes(2)
        group_w(0, 512, nc.vector.tensor_copy)
        group_w(768, 1024, nc.scalar.copy)
        copy_h(0, 0, nc.scalar.copy)
        copy_h(0, 1, nc.scalar.copy)
        group_w(512, 768, nc.vector.tensor_copy)
        copy_h(1, 0, nc.scalar.copy)
        copy_h(1, 1, nc.scalar.copy)
        quantise_w(0)
        quantise_h(0)
        quantise_w(1)
        copy_x(2, 0, nc.scalar.copy)
        copy_x(2, 1, nc.scalar.copy)
        nc.vector.tensor_copy(out=prob[:], in_=prob_bf[:])
        quantise_x(2)
        for n in range(0, PAIRS):
            stage2(n)
            if n == PAIRS - 2:
                keep_clock(4, late=True)
            if n == 0:
                transposes(3)
            elif has(n + 1):
                copy_h(n + 1, 1, nc.scalar.copy)
            if has(n + 2):
                stage1(n + 2)
            if has(n + 3):
                copy_x(n + 3, 0, nc.scalar.copy)
                copy_x(n + 3, 1, nc.scalar.copy)
            if has(n + 4):
                transposes(n + 4)
            bank_max(2 * n, 0)
            bank_max(2 * n, 1)
            if not has(n + 1):
                row_sum(n - 1, [0, 1])
            bank_max(2 * n + 1, 0)
            join_max(2 * n)
            if not has(n + 1):
                invert(n - 1, [0, 1])
                scale(n - 1, 0, nc.gpsimd)
            bank_max(2 * n + 1, 1)
            exponent(2 * n)
            if has(n - 1) and has(n + 1):
                row_sum(n - 1, [0, 1])
            if has(n + 1):
                quantise_h(n + 1)
            join_max(2 * n + 1)
            exponent(2 * n + 1)
            if has(n - 1) and has(n + 1):
                invert(n - 1, [0, 1])
            if has(n + 3):
                quantise_x(n + 3)
            if has(n - 1) and has(n + 1):
                scale(n - 1, 0, nc.gpsimd)
                scale(n - 1, 1, nc.gpsimd)
            if has(n + 2):
                copy_h(n + 2, 0, nc.vector.tensor_copy)
        scale(PAIRS - 2, 1, nc.vector)
        for a in range(2):
            row_sum(PAIRS - 1, [a])
            invert(PAIRS - 1, [a])
            scale(PAIRS - 1, a, nc.vector, 2)
